import numpy as np
import ml_dtypes


def mxq(x, axis, fmt="e4m3"):
    dtype, down = {"e4m3": (ml_dtypes.float8_e4m3fn, 7), "e5m2": (ml_dtypes.float8_e5m2, 14)}[fmt]
    v = np.moveaxis(np.asarray(x, np.float32).astype(ml_dtypes.bfloat16).astype(np.float64), axis, -1)
    blocks = v.reshape(v.shape[:-1] + (-1, 32))
    amax = np.abs(blocks).max(-1, keepdims=True)
    byte = np.maximum(np.where(amax > 0, np.frexp(amax)[1] - 1 + 127, 0) - down, 1)
    scale = np.exp2(byte - 127.0)
    codes = (blocks / scale).astype(np.float32).astype(dtype).astype(np.float64)
    return np.moveaxis((codes * scale).reshape(v.shape), -1, axis)


WIDE = False


def mx_kscale(k):
    if not WIDE:
        return np.ones(k)
    levels = np.array([10, -10, 5, -5, 0])
    a = np.random.permutation(np.resize(levels, k // 512 * 4)).reshape(k // 512, 4)
    idx = np.arange(k)
    return np.exp2(a[idx // 512, idx % 128 // 32])


BF16 = ml_dtypes.bfloat16


def bf(x):
    return np.asarray(x, np.float32).astype(BF16)


def f64(x):
    return np.asarray(x).astype(np.float64)


NU, NI, D = 1024, 1024, 512
N = NU + NI


def setup_inputs():
    s, t = mx_kscale(N), mx_kscale(D)
    return {"A": bf(np.random.uniform(0.0, 2.0 / np.sqrt(N), (N, N)) * s),
            "features": bf(np.random.standard_normal((N, D)) / s[:, None] * t),
            "Wg": bf(np.random.standard_normal((D, D)) / np.sqrt(D) / t[:, None]),
            "bg": bf(np.random.standard_normal(D) * 0.1)}


def reference(A, features, Wg, bg):
    agg = mxq(f64(A), 1, "e4m3") @ mxq(f64(features), 0, "e4m3")
    return np.maximum((mxq(agg, 1, "e4m3") @ mxq(f64(Wg), 0, "e4m3")) + f64(bg), 0.0)

@@ -1,0 +1,233 @@
+from contextlib import ExitStack
+
+import concourse.mybir as mybir
+from concourse.masks import make_identity
+
+F32 = mybir.dt.float32
+BF16 = mybir.dt.bfloat16
+U32 = mybir.dt.uint32
+U8 = mybir.dt.uint8
+FP8X4 = mybir.dt.float8_e4m3fn_x4
+
+P = 128
+PACK = 4
+K_PASS = P * PACK
+NODES = 2048
+FEAT = 512
+A_PASSES = NODES // K_PASS
+FEAT_BLOCKS = FEAT // P
+NODE_TILES = NODES // P
+TILES_PER_ROUND = 2
+ROUNDS = NODE_TILES // TILES_PER_ROUND
+AHEAD = 2
+WORD_BLOCKS_PER_BANK = 4
+BANKS_PER_TILE = NODES // 2 // P // WORD_BLOCKS_PER_BANK
+
+FLOPS = 2 * NODES * NODES * FEAT + 2 * NODES * FEAT * FEAT
+
+
+def tile_net_pa_kernel(tc, A, features, Wg, bg, out):
+    nc = tc.nc
+    with ExitStack() as ctx:
+        keep = ctx.enter_context(tc.tile_pool(name="keep", bufs=1))
+        a_pool = ctx.enter_context(tc.tile_pool(name="a_rows", bufs=NODE_TILES))
+        raw_pool = ctx.enter_context(tc.tile_pool(name="raw", bufs=A_PASSES + 1))
+        regroup_pool = ctx.enter_context(tc.tile_pool(name="regroup", bufs=2))
+        stream = ctx.enter_context(tc.tile_pool(name="stream", bufs=2 * TILES_PER_ROUND))
+        per_round = ctx.enter_context(tc.tile_pool(name="per_round", bufs=2))
+        result_pool = ctx.enter_context(tc.tile_pool(name="result", bufs=3))
+        xt_pool = ctx.enter_context(
+            tc.psum_pool(name="xt", bufs=TILES_PER_ROUND * BANKS_PER_TILE)
+        )
+        agg_pool = ctx.enter_context(tc.psum_pool(name="agg", bufs=TILES_PER_ROUND))
+        out_pool = ctx.enter_context(tc.psum_pool(name="outp", bufs=TILES_PER_ROUND))
+        ctx.enter_context(tc.manual_schedule())
+
+        a_view = A.rearrange("(i p s) k -> i s p k", p=P, s=TILES_PER_ROUND)
+        out_view = out.rearrange("(i p s) e -> i p s e", p=P, s=TILES_PER_ROUND)
+
+        bias_row = keep.tile([P, FEAT], BF16)
+        nc.vector.memset(bias_row[:], 0.0)
+        nc.scalar.dma_start(out=bias_row[0:1, :], in_=bg.unsqueeze(0))
+
+        f_raw = []
+        for g in range(A_PASSES):
+            raw = raw_pool.tile([P, PACK, FEAT], BF16, name="f_raw%d" % g, tag="raw")
+            nc.sync.dma_start(
+                out=raw[:].rearrange("p (u e) c -> p u e c", e=2),
+                in_=features[g * K_PASS : (g + 1) * K_PASS, :].rearrange(
+                    "(u p e) c -> p u e c", p=P, e=2
+                ),
+            )
+            f_raw.append(raw)
+
+        a_rows = []
+
+        def load_a_round(i):
+            for s in range(TILES_PER_ROUND):
+                rows = a_pool.tile([P, NODES], BF16, name="a_rows%d_%d" % (i, s), tag="a_rows")
+                nc.sync.dma_start(out=rows[:], in_=a_view[i, s])
+                a_rows.append(rows)
+
+        for i in range(AHEAD):
+            load_a_round(i)
+        w_raw = raw_pool.tile([P, PACK, FEAT], BF16, name="w_raw", tag="raw")
+        nc.sync.dma_start(out=w_raw[:], in_=Wg.rearrange("(t p) n -> p t n", p=P))
+        for i in range(AHEAD, ROUNDS):
+            load_a_round(i)
+
+        ident = keep.tile([P, P], F32)
+        make_identity(nc, ident[:])
+        ones = keep.tile([P, P], BF16)
+        nc.vector.memset(ones[:], 1.0)
+        bias_psum = out_pool.tile([P, FEAT], F32, name="bias_psum", tag="out_psum")
+        nc.tensor.matmul(out=bias_psum[:], lhsT=ones[:], rhs=bias_row[:], start=True, stop=True)
+        bias = keep.tile([P, FEAT], F32)
+        nc.scalar.copy(out=bias[:], in_=bias_psum[:])
+
+        f_codes = keep.tile([P, A_PASSES, FEAT], U32, align_bytes=64)
+        f_scales = keep.tile([P, A_PASSES, FEAT], U8, align_bytes=64)
+        w_codes = keep.tile([P, FEAT], U32, align_bytes=64)
+        w_scales = keep.tile([P, FEAT], U8, align_bytes=64)
+
+        def regroup(raw, name):
+            grouped = regroup_pool.tile([P, FEAT, PACK], BF16, name=name, tag="grouped", align_bytes=64)
+            half = FEAT // 2
+            nc.vector.tensor_copy(
+                out=grouped[:, :half, :].rearrange("p (c i) t -> p c t i", i=4),
+                in_=raw[:, :, :half].rearrange("p t (c i) -> p c t i", i=4),
+            )
+            nc.scalar.copy(
+                out=grouped[:, half:, :].rearrange("p (c i) t -> p c t i", i=4),
+                in_=raw[:, :, half:].rearrange("p t (c i) -> p c t i", i=4),
+            )
+            return grouped
+
+        def quantise(grouped, codes, scales):
+            nc.vector.quantize_mx(
+                out=codes.bitcast(FP8X4),
+                scales=scales,
+                in_=grouped[:].rearrange("p c t -> p (c t)"),
+            )
+
+        f_grouped = []
+        for g in range(A_PASSES):
+            f_grouped.append(regroup(f_raw[g], "f_grouped%d" % g))
+            if g >= 1:
+                quantise(f_grouped[g - 1], f_codes[:, g - 1, :], f_scales[:, g - 1, :])
+        quantise(f_grouped[A_PASSES - 1], f_codes[:, A_PASSES - 1, :], f_scales[:, A_PASSES - 1, :])
+
+        a_grouped = {}
+        a_codes = {}
+        a_scales = {}
+        agg_grouped = {}
+        agg_codes = {}
+        agg_scales = {}
+        result = {}
+
+        def transpose_a(i):
+            banks = []
+            for s in range(TILES_PER_ROUND):
+                words = a_rows[i * TILES_PER_ROUND + s][:].bitcast(F32)
+                for h in range(BANKS_PER_TILE):
+                    xt = xt_pool.tile([P, WORD_BLOCKS_PER_BANK, P], F32, name="xt")
+                    for b in range(WORD_BLOCKS_PER_BANK):
+                        first = (h * WORD_BLOCKS_PER_BANK + b) * P
+                        nc.tensor.transpose(xt[:, b, :], words[:, first : first + P], ident[:])
+                    banks.append(xt)
+            passes_per_bank = WORD_BLOCKS_PER_BANK // 2
+            for s in range(TILES_PER_ROUND):
+                grouped = stream.tile([P, A_PASSES * P * PACK], BF16, name="a_grouped", align_bytes=64)
+                grouped_words = grouped[:].bitcast(F32).rearrange(
+                    "p (g r u) -> p g r u", g=A_PASSES, u=2
+                )
+                for h in range(BANKS_PER_TILE):
+                    copy = nc.scalar.copy if h % 2 == 0 else nc.vector.tensor_copy
+                    copy(
+                        out=grouped_words[:, h * passes_per_bank : (h + 1) * passes_per_bank],
+                        in_=banks[s * BANKS_PER_TILE + h][:].rearrange("p (g u) r -> p g r u", u=2),
+                    )
+                a_grouped[(i, s)] = grouped
+
+        def quantise_a(i):
+            for s in range(TILES_PER_ROUND):
+                codes = stream.tile([P, A_PASSES * P], U32, name="a_codes", align_bytes=64)
+                scales = stream.tile([P, A_PASSES * P], U8, name="a_scales", align_bytes=64)
+                nc.vector.quantize_mx(
+                    out=codes[:].bitcast(FP8X4), scales=scales[:], in_=a_grouped[(i, s)][:]
+                )
+                a_codes[(i, s)] = codes
+                a_scales[(i, s)] = scales
+
+        def aggregate(i):
+            grouped = per_round.tile([P, TILES_PER_ROUND, P, PACK], BF16, name="agg_grouped", align_bytes=64)
+            for s in range(TILES_PER_ROUND):
+                agg = agg_pool.tile([P, FEAT_BLOCKS, P], F32, name="agg")
+                for t in range(FEAT_BLOCKS):
+                    for g in range(A_PASSES):
+                        nc.tensor.matmul_mx(
+                            out=agg[:, t, :],
+                            lhsT=f_codes[:, g, t * P : (t + 1) * P].bitcast(FP8X4),
+                            lhsT_scale=f_scales[:, g, t * P : (t + 1) * P],
+                            rhs=a_codes[(i, s)][:, g * P : (g + 1) * P].bitcast(FP8X4),
+                            rhs_scale=a_scales[(i, s)][:, g * P : (g + 1) * P],
+                            start=(g == 0),
+                            stop=(g == A_PASSES - 1),
+                        )
+                nc.scalar.copy(out=grouped[:, s, :, :], in_=agg[:].rearrange("p t n -> p n t"))
+            agg_grouped[i] = grouped
+
+        def quantise_agg(i):
+            codes = per_round.tile([P, TILES_PER_ROUND * P], U32, name="agg_codes", align_bytes=64)
+            scales = per_round.tile([P, TILES_PER_ROUND * P], U8, name="agg_scales", align_bytes=64)
+            nc.vector.quantize_mx(
+                out=codes[:].bitcast(FP8X4),
+                scales=scales[:],
+                in_=agg_grouped[i][:].rearrange("p s n t -> p (s n t)"),
+            )
+            agg_codes[i] = codes
+            agg_scales[i] = scales
+
+        def project(i):
+            res = result_pool.tile([P, TILES_PER_ROUND, FEAT], F32, name="result")
+            for s in range(TILES_PER_ROUND):
+                out_psum = out_pool.tile([P, FEAT], F32, name="out_psum")
+                nc.tensor.matmul_mx(
+                    out=out_psum[:],
+                    lhsT=agg_codes[i][:, s * P : (s + 1) * P].bitcast(FP8X4),
+                    lhsT_scale=agg_scales[i][:, s * P : (s + 1) * P],
+                    rhs=w_codes[:].bitcast(FP8X4),
+                    rhs_scale=w_scales[:],
+                    start=True,
+                    stop=True,
+                )
+                nc.vector.tensor_tensor(
+                    out=res[:, s, :], in0=out_psum[:], in1=bias[:], op=mybir.AluOpType.add
+                )
+            result[i] = res
+
+        def finish(i):
+            nc.scalar.activation(
+                out=result[i][:], in_=result[i][:], func=mybir.ActivationFunctionType.Relu
+            )
+            nc.sync.dma_start(out=out_view[i], in_=result[i][:])
+
+        transpose_a(0)
+        quantise_a(0)
+        for i in range(1, AHEAD):
+            transpose_a(i)
+        quantise(regroup(w_raw, "w_grouped"), w_codes[:], w_scales[:])
+
+        for i in range(ROUNDS + 1):
+            if i + 1 < ROUNDS:
+                quantise_a(i + 1)
+            if i < ROUNDS:
+                aggregate(i)
+            if i >= 1:
+                project(i - 1)
+            if i < ROUNDS:
+                quantise_agg(i)
+            if i + AHEAD < ROUNDS:
+                transpose_a(i + AHEAD)
+            if i >= 1:
+                finish(i - 1)

@@ -20,8 +20,11 @@ NODE_TILES = NODES // P
 TILES_PER_ROUND = 2
 ROUNDS = NODE_TILES // TILES_PER_ROUND
 AHEAD = 2
-WORD_BLOCKS_PER_BANK = 4
-BANKS_PER_TILE = NODES // 2 // P // WORD_BLOCKS_PER_BANK
+PLANES_PER_BANK = 4
+BANKS_PER_TILE = NODES // 2 // P // PLANES_PER_BANK
+XT_BANKS = 4
+AGG_BANKS = 2
+OUT_BANKS = 2
 
 FLOPS = 2 * NODES * NODES * FEAT + 2 * NODES * FEAT * FEAT
 
@@ -34,17 +37,10 @@ def tile_net_pa_kernel(tc, A, features, Wg, bg, out):
         raw_pool = ctx.enter_context(tc.tile_pool(name="raw", bufs=A_PASSES + 1))
         regroup_pool = ctx.enter_context(tc.tile_pool(name="regroup", bufs=2))
         stream = ctx.enter_context(tc.tile_pool(name="stream", bufs=2 * TILES_PER_ROUND))
-        per_round = ctx.enter_context(tc.tile_pool(name="per_round", bufs=2))
-        result_pool = ctx.enter_context(tc.tile_pool(name="result", bufs=3))
-        xt_pool = ctx.enter_context(
-            tc.psum_pool(name="xt", bufs=TILES_PER_ROUND * BANKS_PER_TILE)
-        )
-        agg_pool = ctx.enter_context(tc.psum_pool(name="agg", bufs=TILES_PER_ROUND))
-        out_pool = ctx.enter_context(tc.psum_pool(name="outp", bufs=TILES_PER_ROUND))
+        xt_pool = ctx.enter_context(tc.psum_pool(name="xt", bufs=XT_BANKS))
+        agg_pool = ctx.enter_context(tc.psum_pool(name="agg", bufs=AGG_BANKS))
+        out_pool = ctx.enter_context(tc.psum_pool(name="outp", bufs=OUT_BANKS))
         ctx.enter_context(tc.manual_schedule())
-
-        a_view = A.rearrange("(i p s) k -> i s p k", p=P, s=TILES_PER_ROUND)
-        out_view = out.rearrange("(i p s) e -> i p s e", p=P, s=TILES_PER_ROUND)
 
         bias_row = keep.tile([P, FEAT], BF16)
         nc.vector.memset(bias_row[:], 0.0)
@@ -63,27 +59,22 @@ def tile_net_pa_kernel(tc, A, features, Wg, bg, out):
 
         a_rows = []
 
-        def load_a_round(i):
-            for s in range(TILES_PER_ROUND):
-                rows = a_pool.tile([P, NODES], BF16, name="a_rows%d_%d" % (i, s), tag="a_rows")
-                nc.sync.dma_start(out=rows[:], in_=a_view[i, s])
-                a_rows.append(rows)
+        def load_a(j):
+            rows = a_pool.tile([P, NODES], BF16, name="a_rows%d" % j, tag="a_rows")
+            nc.sync.dma_start(out=rows[:], in_=A[j * P : (j + 1) * P, :])
+            a_rows.append(rows)
 
-        for i in range(AHEAD):
-            load_a_round(i)
+        for j in range(AHEAD * TILES_PER_ROUND):
+            load_a(j)
         w_raw = raw_pool.tile([P, PACK, FEAT], BF16, name="w_raw", tag="raw")
         nc.sync.dma_start(out=w_raw[:], in_=Wg.rearrange("(t p) n -> p t n", p=P))
-        for i in range(AHEAD, ROUNDS):
-            load_a_round(i)
+        for j in range(AHEAD * TILES_PER_ROUND, NODE_TILES):
+            load_a(j)
 
         ident = keep.tile([P, P], F32)
         make_identity(nc, ident[:])
         ones = keep.tile([P, P], BF16)
         nc.vector.memset(ones[:], 1.0)
-        bias_psum = out_pool.tile([P, FEAT], F32, name="bias_psum", tag="out_psum")
-        nc.tensor.matmul(out=bias_psum[:], lhsT=ones[:], rhs=bias_row[:], start=True, stop=True)
-        bias = keep.tile([P, FEAT], F32)
-        nc.scalar.copy(out=bias[:], in_=bias_psum[:])
 
         f_codes = keep.tile([P, A_PASSES, FEAT], U32, align_bytes=64)
         f_scales = keep.tile([P, A_PASSES, FEAT], U8, align_bytes=64)
@@ -91,7 +82,9 @@ def tile_net_pa_kernel(tc, A, features, Wg, bg, out):
         w_scales = keep.tile([P, FEAT], U8, align_bytes=64)
 
         def regroup(raw, name):
-            grouped = regroup_pool.tile([P, FEAT, PACK], BF16, name=name, tag="grouped", align_bytes=64)
+            grouped = regroup_pool.tile(
+                [P, FEAT, PACK], BF16, name=name, tag="grouped", align_bytes=64
+            )
             half = FEAT // 2
             nc.vector.tensor_copy(
                 out=grouped[:, :half, :].rearrange("p (c i) t -> p c t i", i=4),
@@ -120,114 +113,104 @@ def tile_net_pa_kernel(tc, A, features, Wg, bg, out):
         a_grouped = {}
         a_codes = {}
         a_scales = {}
-        agg_grouped = {}
         agg_codes = {}
         agg_scales = {}
-        result = {}
 
-        def transpose_a(i):
-            banks = []
-            for s in range(TILES_PER_ROUND):
-                words = a_rows[i * TILES_PER_ROUND + s][:].bitcast(F32)
-                for h in range(BANKS_PER_TILE):
-                    xt = xt_pool.tile([P, WORD_BLOCKS_PER_BANK, P], F32, name="xt")
-                    for b in range(WORD_BLOCKS_PER_BANK):
-                        first = (h * WORD_BLOCKS_PER_BANK + b) * P
-                        nc.tensor.transpose(xt[:, b, :], words[:, first : first + P], ident[:])
-                    banks.append(xt)
-            passes_per_bank = WORD_BLOCKS_PER_BANK // 2
-            for s in range(TILES_PER_ROUND):
-                grouped = stream.tile([P, A_PASSES * P * PACK], BF16, name="a_grouped", align_bytes=64)
-                grouped_words = grouped[:].bitcast(F32).rearrange(
-                    "p (g r u) -> p g r u", g=A_PASSES, u=2
+        def transpose_a(j):
+            words = a_rows[j][:].bitcast(F32)
+            grouped = stream.tile([P, A_PASSES * P * PACK], BF16, name="a_grouped", align_bytes=64)
+            grouped_words = grouped[:].bitcast(F32).rearrange(
+                "p (g r u) -> p g r u", g=A_PASSES, u=2
+            )
+            passes_per_bank = PLANES_PER_BANK // 2
+            for h in range(BANKS_PER_TILE):
+                xt = xt_pool.tile([P, PLANES_PER_BANK, P], F32, name="xt")
+                for b in range(PLANES_PER_BANK):
+                    first = (h * PLANES_PER_BANK + b) * P
+                    nc.tensor.transpose(xt[:, b, :], words[:, first : first + P], ident[:])
+                copy = nc.scalar.copy if h % 2 == 0 else nc.vector.tensor_copy
+                copy(
+                    out=grouped_words[:, h * passes_per_bank : (h + 1) * passes_per_bank],
+                    in_=xt[:].rearrange("p (g u) r -> p g r u", u=2),
                 )
-                for h in range(BANKS_PER_TILE):
-                    copy = nc.scalar.copy if h % 2 == 0 else nc.vector.tensor_copy
-                    copy(
-                        out=grouped_words[:, h * passes_per_bank : (h + 1) * passes_per_bank],
-                        in_=banks[s * BANKS_PER_TILE + h][:].rearrange("p (g u) r -> p g r u", u=2),
-                    )
-                a_grouped[(i, s)] = grouped
+            a_grouped[j] = grouped
 
-        def quantise_a(i):
-            for s in range(TILES_PER_ROUND):
-                codes = stream.tile([P, A_PASSES * P], U32, name="a_codes", align_bytes=64)
-                scales = stream.tile([P, A_PASSES * P], U8, name="a_scales", align_bytes=64)
-                nc.vector.quantize_mx(
-                    out=codes[:].bitcast(FP8X4), scales=scales[:], in_=a_grouped[(i, s)][:]
-                )
-                a_codes[(i, s)] = codes
-                a_scales[(i, s)] = scales
-
-        def aggregate(i):
-            grouped = per_round.tile([P, TILES_PER_ROUND, P, PACK], BF16, name="agg_grouped", align_bytes=64)
-            for s in range(TILES_PER_ROUND):
-                agg = agg_pool.tile([P, FEAT_BLOCKS, P], F32, name="agg")
-                for t in range(FEAT_BLOCKS):
-                    for g in range(A_PASSES):
-                        nc.tensor.matmul_mx(
-                            out=agg[:, t, :],
-                            lhsT=f_codes[:, g, t * P : (t + 1) * P].bitcast(FP8X4),
-                            lhsT_scale=f_scales[:, g, t * P : (t + 1) * P],
-                            rhs=a_codes[(i, s)][:, g * P : (g + 1) * P].bitcast(FP8X4),
-                            rhs_scale=a_scales[(i, s)][:, g * P : (g + 1) * P],
-                            start=(g == 0),
-                            stop=(g == A_PASSES - 1),
-                        )
-                nc.scalar.copy(out=grouped[:, s, :, :], in_=agg[:].rearrange("p t n -> p n t"))
-            agg_grouped[i] = grouped
-
-        def quantise_agg(i):
-            codes = per_round.tile([P, TILES_PER_ROUND * P], U32, name="agg_codes", align_bytes=64)
-            scales = per_round.tile([P, TILES_PER_ROUND * P], U8, name="agg_scales", align_bytes=64)
+        def quantise_a(j):
+            codes = stream.tile([P, A_PASSES * P], U32, name="a_codes", align_bytes=64)
+            scales = stream.tile([P, A_PASSES * P], U8, name="a_scales", align_bytes=64)
             nc.vector.quantize_mx(
-                out=codes[:].bitcast(FP8X4),
-                scales=scales[:],
-                in_=agg_grouped[i][:].rearrange("p s n t -> p (s n t)"),
+                out=codes[:].bitcast(FP8X4), scales=scales[:], in_=a_grouped[j][:]
             )
-            agg_codes[i] = codes
-            agg_scales[i] = scales
+            a_codes[j] = codes
+            a_scales[j] = scales
 
-        def project(i):
-            res = result_pool.tile([P, TILES_PER_ROUND, FEAT], F32, name="result")
-            for s in range(TILES_PER_ROUND):
-                out_psum = out_pool.tile([P, FEAT], F32, name="out_psum")
-                nc.tensor.matmul_mx(
-                    out=out_psum[:],
-                    lhsT=agg_codes[i][:, s * P : (s + 1) * P].bitcast(FP8X4),
-                    lhsT_scale=agg_scales[i][:, s * P : (s + 1) * P],
-                    rhs=w_codes[:].bitcast(FP8X4),
-                    rhs_scale=w_scales[:],
-                    start=True,
-                    stop=True,
-                )
-                nc.vector.tensor_tensor(
-                    out=res[:, s, :], in0=out_psum[:], in1=bias[:], op=mybir.AluOpType.add
-                )
-            result[i] = res
+        def aggregate(j):
+            agg = agg_pool.tile([P, FEAT_BLOCKS, P], F32, name="agg")
+            for t in range(FEAT_BLOCKS):
+                for g in range(A_PASSES):
+                    nc.tensor.matmul_mx(
+                        out=agg[:, t, :],
+                        lhsT=f_codes[:, g, t * P : (t + 1) * P].bitcast(FP8X4),
+                        lhsT_scale=f_scales[:, g, t * P : (t + 1) * P],
+                        rhs=a_codes[j][:, g * P : (g + 1) * P].bitcast(FP8X4),
+                        rhs_scale=a_scales[j][:, g * P : (g + 1) * P],
+                        start=(g == 0),
+                        stop=(g == A_PASSES - 1),
+                    )
+            grouped = stream.tile([P, P, PACK], BF16, name="agg_grouped", align_bytes=64)
+            nc.scalar.copy(out=grouped[:], in_=agg[:].rearrange("p t n -> p n t"))
+            codes = stream.tile([P, P], U32, name="agg_codes", align_bytes=64)
+            scales = stream.tile([P, P], U8, name="agg_scales", align_bytes=64)
+            quantise(grouped, codes[:], scales[:])
+            agg_codes[j] = codes
+            agg_scales[j] = scales
 
-        def finish(i):
+        def project(j):
+            out_psum = out_pool.tile([P, FEAT], F32, name="out_psum")
+            nc.tensor.matmul_mx(
+                out=out_psum[:],
+                lhsT=agg_codes[j][:].bitcast(FP8X4),
+                lhsT_scale=agg_scales[j][:],
+                rhs=w_codes[:].bitcast(FP8X4),
+                rhs_scale=w_scales[:],
+                start=True,
+                stop=True,
+            )
+            result = stream.tile([P, FEAT], F32, name="result")
+            nc.vector.tensor_tensor(
+                out=result[:], in0=out_psum[:], in1=bias[:], op=mybir.AluOpType.add
+            )
             nc.scalar.activation(
-                out=result[i][:], in_=result[i][:], func=mybir.ActivationFunctionType.Relu
+                out=result[:], in_=result[:], func=mybir.ActivationFunctionType.Relu
             )
-            nc.sync.dma_start(out=out_view[i], in_=result[i][:])
+            nc.sync.dma_start(out=out[j * P : (j + 1) * P, :], in_=result[:])
 
-        transpose_a(0)
-        quantise_a(0)
+        def tiles_of(i):
+            return range(i * TILES_PER_ROUND, (i + 1) * TILES_PER_ROUND)
+
+        for j in tiles_of(0):
+            transpose_a(j)
+        for j in tiles_of(0):
+            quantise_a(j)
         for i in range(1, AHEAD):
-            transpose_a(i)
+            for j in tiles_of(i):
+                transpose_a(j)
+        bias_psum = out_pool.tile([P, FEAT], F32, name="bias_psum", tag="out_psum")
+        nc.tensor.matmul(out=bias_psum[:], lhsT=ones[:], rhs=bias_row[:], start=True, stop=True)
+        bias = keep.tile([P, FEAT], F32)
+        nc.scalar.copy(out=bias[:], in_=bias_psum[:])
         quantise(regroup(w_raw, "w_grouped"), w_codes[:], w_scales[:])
 
         for i in range(ROUNDS + 1):
             if i + 1 < ROUNDS:
-                quantise_a(i + 1)
+                for j in tiles_of(i + 1):
+                    quantise_a(j)
             if i < ROUNDS:
-                aggregate(i)
+                for j in tiles_of(i):
+                    aggregate(j)
             if i >= 1:
-                project(i - 1)
-            if i < ROUNDS:
-                quantise_agg(i)
+                for j in tiles_of(i - 1):
+                    project(j)
             if i + AHEAD < ROUNDS:
-                transpose_a(i + AHEAD)
-            if i >= 1:
-                finish(i - 1)
+                for j in tiles_of(i + AHEAD):
+                    transpose_a(j)

@@ -128,8 +128,7 @@ def tile_net_pa_kernel(tc, A, features, Wg, bg, out):
                 for b in range(PLANES_PER_BANK):
                     first = (h * PLANES_PER_BANK + b) * P
                     nc.tensor.transpose(xt[:, b, :], words[:, first : first + P], ident[:])
-                copy = nc.scalar.copy if h % 2 == 0 else nc.vector.tensor_copy
-                copy(
+                nc.scalar.copy(
                     out=grouped_words[:, h * passes_per_bank : (h + 1) * passes_per_bank],
                     in_=xt[:].rearrange("p (g u) r -> p g r u", u=2),
                 )
@@ -165,6 +164,8 @@ def tile_net_pa_kernel(tc, A, features, Wg, bg, out):
             agg_codes[j] = codes
             agg_scales[j] = scales
 
+        result = {}
+
         def project(j):
             out_psum = out_pool.tile([P, FEAT], F32, name="out_psum")
             nc.tensor.matmul_mx(
@@ -176,14 +177,14 @@ def tile_net_pa_kernel(tc, A, features, Wg, bg, out):
                 start=True,
                 stop=True,
             )
-            result = stream.tile([P, FEAT], F32, name="result")
+            result[j] = stream.tile([P, FEAT], F32, name="result")
             nc.vector.tensor_tensor(
-                out=result[:], in0=out_psum[:], in1=bias[:], op=mybir.AluOpType.add
+                out=result[j][:], in0=out_psum[:], in1=bias[:], op=mybir.AluOpType.add
             )
-            nc.scalar.activation(
-                out=result[:], in_=result[:], func=mybir.ActivationFunctionType.Relu
-            )
-            nc.sync.dma_start(out=out[j * P : (j + 1) * P, :], in_=result[:])
+
+        def finish(j):
+            nc.vector.tensor_scalar_max(out=result[j][:], in0=result[j][:], scalar1=0.0)
+            nc.sync.dma_start(out=out[j * P : (j + 1) * P, :], in_=result[j][:])
 
         def tiles_of(i):
             return range(i * TILES_PER_ROUND, (i + 1) * TILES_PER_ROUND)
@@ -211,6 +212,8 @@ def tile_net_pa_kernel(tc, A, features, Wg, bg, out):
             if i >= 1:
                 for j in tiles_of(i - 1):
                     project(j)
+                for j in tiles_of(i - 1):
+                    finish(j)
             if i + AHEAD < ROUNDS:
                 for j in tiles_of(i + AHEAD):
                     transpose_a(j)

@@ -18,12 +18,14 @@ A_PASSES = NODES // K_PASS
 FEAT_BLOCKS = FEAT // P
 NODE_TILES = NODES // P
 TILES_PER_ROUND = 2
+ROUND_NODES = TILES_PER_ROUND * P
 ROUNDS = NODE_TILES // TILES_PER_ROUND
 AHEAD = 2
 PLANES_PER_BANK = 4
 BANKS_PER_TILE = NODES // 2 // P // PLANES_PER_BANK
 XT_BANKS = 4
 AGG_BANKS = 2
+BLOCKS_PER_BANK = FEAT_BLOCKS // AGG_BANKS
 OUT_BANKS = 2
 
 FLOPS = 2 * NODES * NODES * FEAT + 2 * NODES * FEAT * FEAT
@@ -36,7 +38,8 @@ def tile_net_pa_kernel(tc, A, features, Wg, bg, out):
         a_pool = ctx.enter_context(tc.tile_pool(name="a_rows", bufs=NODE_TILES))
         raw_pool = ctx.enter_context(tc.tile_pool(name="raw", bufs=A_PASSES + 1))
         regroup_pool = ctx.enter_context(tc.tile_pool(name="regroup", bufs=2))
-        stream = ctx.enter_context(tc.tile_pool(name="stream", bufs=2 * TILES_PER_ROUND))
+        stream = ctx.enter_context(tc.tile_pool(name="stream", bufs=2))
+        result_pool = ctx.enter_context(tc.tile_pool(name="result", bufs=2 * TILES_PER_ROUND))
         xt_pool = ctx.enter_context(tc.psum_pool(name="xt", bufs=XT_BANKS))
         agg_pool = ctx.enter_context(tc.psum_pool(name="agg", bufs=AGG_BANKS))
         out_pool = ctx.enter_context(tc.psum_pool(name="outp", bufs=OUT_BANKS))
@@ -115,69 +118,83 @@ def tile_net_pa_kernel(tc, A, features, Wg, bg, out):
         a_scales = {}
         agg_codes = {}
         agg_scales = {}
+        passes_per_bank = PLANES_PER_BANK // 2
+        bank_columns = passes_per_bank * ROUND_NODES
 
-        def transpose_a(j):
-            words = a_rows[j][:].bitcast(F32)
-            grouped = stream.tile([P, A_PASSES * P * PACK], BF16, name="a_grouped", align_bytes=64)
+        def transpose_a(i):
+            grouped = stream.tile(
+                [P, A_PASSES * ROUND_NODES * PACK], BF16, name="a_grouped", align_bytes=64
+            )
             grouped_words = grouped[:].bitcast(F32).rearrange(
-                "p (g r u) -> p g r u", g=A_PASSES, u=2
+                "p (g s r u) -> p g s r u", g=A_PASSES, s=TILES_PER_ROUND, u=2
             )
-            passes_per_bank = PLANES_PER_BANK // 2
-            for h in range(BANKS_PER_TILE):
-                xt = xt_pool.tile([P, PLANES_PER_BANK, P], F32, name="xt")
-                for b in range(PLANES_PER_BANK):
-                    first = (h * PLANES_PER_BANK + b) * P
-                    nc.tensor.transpose(xt[:, b, :], words[:, first : first + P], ident[:])
-                nc.scalar.copy(
-                    out=grouped_words[:, h * passes_per_bank : (h + 1) * passes_per_bank],
-                    in_=xt[:].rearrange("p (g u) r -> p g r u", u=2),
-                )
-            a_grouped[j] = grouped
-
-        def quantise_a(j):
-            codes = stream.tile([P, A_PASSES * P], U32, name="a_codes", align_bytes=64)
-            scales = stream.tile([P, A_PASSES * P], U8, name="a_scales", align_bytes=64)
-            nc.vector.quantize_mx(
-                out=codes[:].bitcast(FP8X4), scales=scales[:], in_=a_grouped[j][:]
-            )
-            a_codes[j] = codes
-            a_scales[j] = scales
-
-        def aggregate(j):
-            agg = agg_pool.tile([P, FEAT_BLOCKS, P], F32, name="agg")
-            for t in range(FEAT_BLOCKS):
-                for g in range(A_PASSES):
-                    nc.tensor.matmul_mx(
-                        out=agg[:, t, :],
-                        lhsT=f_codes[:, g, t * P : (t + 1) * P].bitcast(FP8X4),
-                        lhsT_scale=f_scales[:, g, t * P : (t + 1) * P],
-                        rhs=a_codes[j][:, g * P : (g + 1) * P].bitcast(FP8X4),
-                        rhs_scale=a_scales[j][:, g * P : (g + 1) * P],
-                        start=(g == 0),
-                        stop=(g == A_PASSES - 1),
+            for s in range(TILES_PER_ROUND):
+                words = a_rows[i * TILES_PER_ROUND + s][:].bitcast(F32)
+                for h in range(BANKS_PER_TILE):
+                    xt = xt_pool.tile([P, PLANES_PER_BANK, P], F32, name="xt")
+                    for b in range(PLANES_PER_BANK):
+                        first = (h * PLANES_PER_BANK + b) * P
+                        nc.tensor.transpose(xt[:, b, :], words[:, first : first + P], ident[:])
+                    nc.scalar.copy(
+                        out=grouped_words[:, h * passes_per_bank : (h + 1) * passes_per_bank, s],
+                        in_=xt[:].rearrange("p (g u) r -> p g r u", u=2),
                     )
-            grouped = stream.tile([P, P, PACK], BF16, name="agg_grouped", align_bytes=64)
-            nc.scalar.copy(out=grouped[:], in_=agg[:].rearrange("p t n -> p n t"))
-            codes = stream.tile([P, P], U32, name="agg_codes", align_bytes=64)
-            scales = stream.tile([P, P], U8, name="agg_scales", align_bytes=64)
+            a_grouped[i] = grouped
+
+        def quantise_a(i):
+            codes = stream.tile([P, A_PASSES * ROUND_NODES], U32, name="a_codes", align_bytes=64)
+            scales = stream.tile([P, A_PASSES * ROUND_NODES], U8, name="a_scales", align_bytes=64)
+            for h in range(BANKS_PER_TILE):
+                nc.vector.quantize_mx(
+                    out=codes[:, h * bank_columns : (h + 1) * bank_columns].bitcast(FP8X4),
+                    scales=scales[:, h * bank_columns : (h + 1) * bank_columns],
+                    in_=a_grouped[i][:, h * bank_columns * PACK : (h + 1) * bank_columns * PACK],
+                )
+            a_codes[i] = codes
+            a_scales[i] = scales
+
+        def aggregate(i):
+            grouped = stream.tile([P, ROUND_NODES, PACK], BF16, name="agg_grouped", align_bytes=64)
+            for b in range(AGG_BANKS):
+                agg = agg_pool.tile([P, BLOCKS_PER_BANK, ROUND_NODES], F32, name="agg")
+                for t in range(BLOCKS_PER_BANK):
+                    block = (b * BLOCKS_PER_BANK + t) * P
+                    for g in range(A_PASSES):
+                        nc.tensor.matmul_mx(
+                            out=agg[:, t, :],
+                            lhsT=f_codes[:, g, block : block + P].bitcast(FP8X4),
+                            lhsT_scale=f_scales[:, g, block : block + P],
+                            rhs=a_codes[i][:, g * ROUND_NODES : (g + 1) * ROUND_NODES].bitcast(FP8X4),
+                            rhs_scale=a_scales[i][:, g * ROUND_NODES : (g + 1) * ROUND_NODES],
+                            start=(g == 0),
+                            stop=(g == A_PASSES - 1),
+                        )
+                nc.scalar.copy(
+                    out=grouped[:, :, b * BLOCKS_PER_BANK : (b + 1) * BLOCKS_PER_BANK],
+                    in_=agg[:].rearrange("p t n -> p n t"),
+                )
+            codes = stream.tile([P, ROUND_NODES], U32, name="agg_codes", align_bytes=64)
+            scales = stream.tile([P, ROUND_NODES], U8, name="agg_scales", align_bytes=64)
             quantise(grouped, codes[:], scales[:])
-            agg_codes[j] = codes
-            agg_scales[j] = scales
+            agg_codes[i] = codes
+            agg_scales[i] = scales
 
         result = {}
 
         def project(j):
+            first = (j % TILES_PER_ROUND) * P
+            nodes = slice(first, first + P)
             out_psum = out_pool.tile([P, FEAT], F32, name="out_psum")
             nc.tensor.matmul_mx(
                 out=out_psum[:],
-                lhsT=agg_codes[j][:].bitcast(FP8X4),
-                lhsT_scale=agg_scales[j][:],
+                lhsT=agg_codes[j // TILES_PER_ROUND][:, nodes].bitcast(FP8X4),
+                lhsT_scale=agg_scales[j // TILES_PER_ROUND][:, nodes],
                 rhs=w_codes[:].bitcast(FP8X4),
                 rhs_scale=w_scales[:],
                 start=True,
                 stop=True,
             )
-            result[j] = stream.tile([P, FEAT], F32, name="result")
+            result[j] = result_pool.tile([P, FEAT], F32, name="result")
             nc.vector.tensor_tensor(
                 out=result[j][:], in0=out_psum[:], in1=bias[:], op=mybir.AluOpType.add
             )
@@ -189,13 +206,10 @@ def tile_net_pa_kernel(tc, A, features, Wg, bg, out):
         def tiles_of(i):
             return range(i * TILES_PER_ROUND, (i + 1) * TILES_PER_ROUND)
 
-        for j in tiles_of(0):
-            transpose_a(j)
-        for j in tiles_of(0):
-            quantise_a(j)
+        transpose_a(0)
+        quantise_a(0)
         for i in range(1, AHEAD):
-            for j in tiles_of(i):
-                transpose_a(j)
+            transpose_a(i)
         bias_psum = out_pool.tile([P, FEAT], F32, name="bias_psum", tag="out_psum")
         nc.tensor.matmul(out=bias_psum[:], lhsT=ones[:], rhs=bias_row[:], start=True, stop=True)
         bias = keep.tile([P, FEAT], F32)
@@ -204,16 +218,13 @@ def tile_net_pa_kernel(tc, A, features, Wg, bg, out):
 
         for i in range(ROUNDS + 1):
             if i + 1 < ROUNDS:
-                for j in tiles_of(i + 1):
-                    quantise_a(j)
+                quantise_a(i + 1)
             if i < ROUNDS:
-                for j in tiles_of(i):
-                    aggregate(j)
+                aggregate(i)
             if i >= 1:
                 for j in tiles_of(i - 1):
                     project(j)
                 for j in tiles_of(i - 1):
                     finish(j)
             if i + AHEAD < ROUNDS:
-                for j in tiles_of(i + AHEAD):
-                    transpose_a(j)
+                transpose_a(i + AHEAD)

from contextlib import ExitStack

import concourse.mybir as mybir
from concourse.masks import make_identity

F32 = mybir.dt.float32
BF16 = mybir.dt.bfloat16
U32 = mybir.dt.uint32
U8 = mybir.dt.uint8
FP8X4 = mybir.dt.float8_e4m3fn_x4

P = 128
PACK = 4
K_PASS = P * PACK
NODES = 2048
FEAT = 512
A_PASSES = NODES // K_PASS
FEAT_BLOCKS = FEAT // P
NODE_TILES = NODES // P
TILES_PER_ROUND = 2
ROUND_NODES = TILES_PER_ROUND * P
ROUNDS = NODE_TILES // TILES_PER_ROUND
AHEAD = 2
PLANES_PER_BANK = 4
BANKS_PER_TILE = NODES // 2 // P // PLANES_PER_BANK
XT_BANKS = 4
AGG_BANKS = 2
BLOCKS_PER_BANK = FEAT_BLOCKS // AGG_BANKS
OUT_BANKS = 2

FLOPS = 2 * NODES * NODES * FEAT + 2 * NODES * FEAT * FEAT


def tile_net_pa_kernel(tc, A, features, Wg, bg, out):
    nc = tc.nc
    with ExitStack() as ctx:
        keep = ctx.enter_context(tc.tile_pool(name="keep", bufs=1))
        a_pool = ctx.enter_context(tc.tile_pool(name="a_rows", bufs=NODE_TILES))
        raw_pool = ctx.enter_context(tc.tile_pool(name="raw", bufs=A_PASSES + 1))
        regroup_pool = ctx.enter_context(tc.tile_pool(name="regroup", bufs=2))
        stream = ctx.enter_context(tc.tile_pool(name="stream", bufs=2))
        result_pool = ctx.enter_context(tc.tile_pool(name="result", bufs=2 * TILES_PER_ROUND))
        xt_pool = ctx.enter_context(tc.psum_pool(name="xt", bufs=XT_BANKS))
        agg_pool = ctx.enter_context(tc.psum_pool(name="agg", bufs=AGG_BANKS))
        out_pool = ctx.enter_context(tc.psum_pool(name="outp", bufs=OUT_BANKS))
        ctx.enter_context(tc.manual_schedule())

        bias_row = keep.tile([P, FEAT], BF16)
        nc.vector.memset(bias_row[:], 0.0)
        nc.scalar.dma_start(out=bias_row[0:1, :], in_=bg.unsqueeze(0))

        f_raw = []
        for g in range(A_PASSES):
            raw = raw_pool.tile([P, PACK, FEAT], BF16, name="f_raw%d" % g, tag="raw")
            nc.sync.dma_start(
                out=raw[:].rearrange("p (u e) c -> p u e c", e=2),
                in_=features[g * K_PASS : (g + 1) * K_PASS, :].rearrange(
                    "(u p e) c -> p u e c", p=P, e=2
                ),
            )
            f_raw.append(raw)

        a_rows = []

        def load_a(j):
            rows = a_pool.tile([P, NODES], BF16, name="a_rows%d" % j, tag="a_rows")
            nc.sync.dma_start(out=rows[:], in_=A[j * P : (j + 1) * P, :])
            a_rows.append(rows)

        for j in range(AHEAD * TILES_PER_ROUND):
            load_a(j)
        w_raw = raw_pool.tile([P, PACK, FEAT], BF16, name="w_raw", tag="raw")
        nc.sync.dma_start(out=w_raw[:], in_=Wg.rearrange("(t p) n -> p t n", p=P))
        for j in range(AHEAD * TILES_PER_ROUND, NODE_TILES):
            load_a(j)

        ident = keep.tile([P, P], F32)
        make_identity(nc, ident[:])
        ones = keep.tile([P, P], BF16)
        nc.vector.memset(ones[:], 1.0)

        f_codes = keep.tile([P, A_PASSES, FEAT], U32, align_bytes=64)
        f_scales = keep.tile([P, A_PASSES, FEAT], U8, align_bytes=64)
        w_codes = keep.tile([P, FEAT], U32, align_bytes=64)
        w_scales = keep.tile([P, FEAT], U8, align_bytes=64)

        def regroup(raw, name):
            grouped = regroup_pool.tile(
                [P, FEAT, PACK], BF16, name=name, tag="grouped", align_bytes=64
            )
            half = FEAT // 2
            nc.vector.tensor_copy(
                out=grouped[:, :half, :].rearrange("p (c i) t -> p c t i", i=4),
                in_=raw[:, :, :half].rearrange("p t (c i) -> p c t i", i=4),
            )
            nc.scalar.copy(
                out=grouped[:, half:, :].rearrange("p (c i) t -> p c t i", i=4),
                in_=raw[:, :, half:].rearrange("p t (c i) -> p c t i", i=4),
            )
            return grouped

        def quantise(grouped, codes, scales):
            nc.vector.quantize_mx(
                out=codes.bitcast(FP8X4),
                scales=scales,
                in_=grouped[:].rearrange("p c t -> p (c t)"),
            )

        f_grouped = []
        for g in range(A_PASSES):
            f_grouped.append(regroup(f_raw[g], "f_grouped%d" % g))
            if g >= 1:
                quantise(f_grouped[g - 1], f_codes[:, g - 1, :], f_scales[:, g - 1, :])
        quantise(f_grouped[A_PASSES - 1], f_codes[:, A_PASSES - 1, :], f_scales[:, A_PASSES - 1, :])

        a_grouped = {}
        a_codes = {}
        a_scales = {}
        agg_codes = {}
        agg_scales = {}
        passes_per_bank = PLANES_PER_BANK // 2
        bank_columns = passes_per_bank * ROUND_NODES

        def transpose_a(i):
            grouped = stream.tile(
                [P, A_PASSES * ROUND_NODES * PACK], BF16, name="a_grouped", align_bytes=64
            )
            grouped_words = grouped[:].bitcast(F32).rearrange(
                "p (g s r u) -> p g s r u", g=A_PASSES, s=TILES_PER_ROUND, u=2
            )
            for s in range(TILES_PER_ROUND):
                words = a_rows[i * TILES_PER_ROUND + s][:].bitcast(F32)
                for h in range(BANKS_PER_TILE):
                    xt = xt_pool.tile([P, PLANES_PER_BANK, P], F32, name="xt")
                    for b in range(PLANES_PER_BANK):
                        first = (h * PLANES_PER_BANK + b) * P
                        nc.tensor.transpose(xt[:, b, :], words[:, first : first + P], ident[:])
                    nc.scalar.copy(
                        out=grouped_words[:, h * passes_per_bank : (h + 1) * passes_per_bank, s],
                        in_=xt[:].rearrange("p (g u) r -> p g r u", u=2),
                    )
            a_grouped[i] = grouped

        def quantise_a(i):
            codes = stream.tile([P, A_PASSES * ROUND_NODES], U32, name="a_codes", align_bytes=64)
            scales = stream.tile([P, A_PASSES * ROUND_NODES], U8, name="a_scales", align_bytes=64)
            for h in range(BANKS_PER_TILE):
                nc.vector.quantize_mx(
                    out=codes[:, h * bank_columns : (h + 1) * bank_columns].bitcast(FP8X4),
                    scales=scales[:, h * bank_columns : (h + 1) * bank_columns],
                    in_=a_grouped[i][:, h * bank_columns * PACK : (h + 1) * bank_columns * PACK],
                )
            a_codes[i] = codes
            a_scales[i] = scales

        def aggregate(i):
            grouped = stream.tile([P, ROUND_NODES, PACK], BF16, name="agg_grouped", align_bytes=64)
            for b in range(AGG_BANKS):
                agg = agg_pool.tile([P, BLOCKS_PER_BANK, ROUND_NODES], F32, name="agg")
                for t in range(BLOCKS_PER_BANK):
                    block = (b * BLOCKS_PER_BANK + t) * P
                    for g in range(A_PASSES):
                        nc.tensor.matmul_mx(
                            out=agg[:, t, :],
                            lhsT=f_codes[:, g, block : block + P].bitcast(FP8X4),
                            lhsT_scale=f_scales[:, g, block : block + P],
                            rhs=a_codes[i][:, g * ROUND_NODES : (g + 1) * ROUND_NODES].bitcast(FP8X4),
                            rhs_scale=a_scales[i][:, g * ROUND_NODES : (g + 1) * ROUND_NODES],
                            start=(g == 0),
                            stop=(g == A_PASSES - 1),
                        )
                nc.scalar.copy(
                    out=grouped[:, :, b * BLOCKS_PER_BANK : (b + 1) * BLOCKS_PER_BANK],
                    in_=agg[:].rearrange("p t n -> p n t"),
                )
            codes = stream.tile([P, ROUND_NODES], U32, name="agg_codes", align_bytes=64)
            scales = stream.tile([P, ROUND_NODES], U8, name="agg_scales", align_bytes=64)
            quantise(grouped, codes[:], scales[:])
            agg_codes[i] = codes
            agg_scales[i] = scales

        result = {}

        def project(j):
            first = (j % TILES_PER_ROUND) * P
            nodes = slice(first, first + P)
            out_psum = out_pool.tile([P, FEAT], F32, name="out_psum")
            nc.tensor.matmul_mx(
                out=out_psum[:],
                lhsT=agg_codes[j // TILES_PER_ROUND][:, nodes].bitcast(FP8X4),
                lhsT_scale=agg_scales[j // TILES_PER_ROUND][:, nodes],
                rhs=w_codes[:].bitcast(FP8X4),
                rhs_scale=w_scales[:],
                start=True,
                stop=True,
            )
            result[j] = result_pool.tile([P, FEAT], F32, name="result")
            nc.vector.tensor_tensor(
                out=result[j][:], in0=out_psum[:], in1=bias[:], op=mybir.AluOpType.add
            )

        def finish(j):
            nc.vector.tensor_scalar_max(out=result[j][:], in0=result[j][:], scalar1=0.0)
            nc.sync.dma_start(out=out[j * P : (j + 1) * P, :], in_=result[j][:])

        def tiles_of(i):
            return range(i * TILES_PER_ROUND, (i + 1) * TILES_PER_ROUND)

        transpose_a(0)
        quantise_a(0)
        for i in range(1, AHEAD):
            transpose_a(i)
        bias_psum = out_pool.tile([P, FEAT], F32, name="bias_psum", tag="out_psum")
        nc.tensor.matmul(out=bias_psum[:], lhsT=ones[:], rhs=bias_row[:], start=True, stop=True)
        bias = keep.tile([P, FEAT], F32)
        nc.scalar.copy(out=bias[:], in_=bias_psum[:])
        quantise(regroup(w_raw, "w_grouped"), w_codes[:], w_scales[:])

        for i in range(ROUNDS + 1):
            if i + 1 < ROUNDS:
                quantise_a(i + 1)
            if i < ROUNDS:
                aggregate(i)
            if i >= 1:
                for j in tiles_of(i - 1):
                    project(j)
                for j in tiles_of(i - 1):
                    finish(j)
            if i + AHEAD < ROUNDS:
                transpose_a(i + AHEAD)
